import numpy as np
import ml_dtypes


def mxq(x, axis, fmt="e4m3"):
    dtype, down = {"e4m3": (ml_dtypes.float8_e4m3fn, 7), "e5m2": (ml_dtypes.float8_e5m2, 14)}[fmt]
    v = np.moveaxis(np.asarray(x, np.float32).astype(ml_dtypes.bfloat16).astype(np.float64), axis, -1)
    blocks = v.reshape(v.shape[:-1] + (-1, 32))
    amax = np.abs(blocks).max(-1, keepdims=True)
    byte = np.maximum(np.where(amax > 0, np.frexp(amax)[1] - 1 + 127, 0) - down, 1)
    scale = np.exp2(byte - 127.0)
    codes = (blocks / scale).astype(np.float32).astype(dtype).astype(np.float64)
    return np.moveaxis((codes * scale).reshape(v.shape), -1, axis)


WIDE = False


def mx_kscale(k):
    if not WIDE:
        return np.ones(k)
    levels = np.array([10, -10, 5, -5, 0])
    a = np.random.permutation(np.resize(levels, k // 512 * 4)).reshape(k // 512, 4)
    idx = np.arange(k)
    return np.exp2(a[idx // 512, idx % 128 // 32])


BF16 = ml_dtypes.bfloat16


def bf(x):
    return np.asarray(x, np.float32).astype(BF16)


def f64(x):
    return np.asarray(x).astype(np.float64)


E2M1 = np.array([0.0, 0.5, 1.0, 1.5, 2.0, 3.0, 4.0, 6.0, -0.0, -0.5, -1.0, -1.5, -2.0, -3.0, -4.0, -6.0])


def pack_weight(w, fmt):
    k, n = w.shape
    w = f64(bf(w)).reshape(k // 32, 32, n)
    amax = np.abs(w).max(1)
    if fmt == "e4m3":
        byte = np.frexp(amax)[1] - 1 + 127 - 7
    else:
        mant, ex = np.frexp(amax / 6.0)
        byte = np.where(mant > 0.5, ex, ex - 1) + 127
    byte = np.clip(np.where(amax > 0, byte, 1), 1, 254)
    scaled = (w * np.exp2(127.0 - byte)[:, None, :]).reshape(k, n).astype(np.float32)
    by_word = np.ascontiguousarray(scaled.reshape(k // 512, 128, 4, n).transpose(0, 1, 3, 2))
    if fmt == "e4m3":
        words = by_word.astype(ml_dtypes.float8_e4m3fn).view(np.uint8)
    else:
        c = by_word.astype(ml_dtypes.float4_e2m1fn).view(np.uint8) & 0xF
        words = c[..., 0::2] | (c[..., 1::2] << 4)
    return np.ascontiguousarray(words), np.ascontiguousarray(byte.astype(np.uint8).reshape(k // 512, 16, n))


def unpack_weight(words, scales, fmt):
    g, p, n, _ = words.shape
    if fmt == "e4m3":
        vals = np.ascontiguousarray(words).view(ml_dtypes.float8_e4m3fn).astype(np.float64)
    else:
        nib = np.empty((g, p, n, 4), np.uint8)
        nib[..., 0::2] = words & 0xF
        nib[..., 1::2] = words >> 4
        vals = E2M1[nib]
    vals = vals * np.repeat(np.exp2(scales.astype(np.float64) - 127.0), 8, axis=1)[..., None]
    return vals.transpose(0, 1, 3, 2).reshape(g * 512, n)


B, K, D, NK, O = 160, 36, 512, 4, 256


def setup_inputs():
    s = mx_kscale(D)
    neighbourhood_features = bf(np.random.standard_normal((B, K, D)) * s)
    region_relation_weights = bf(np.random.uniform(size=(B, K, K)))
    mean_relation = bf(np.random.uniform(size=NK))
    precision_relation = bf(0.25 + 0.75 * np.random.uniform(size=NK))
    stack = np.random.standard_normal((NK, O, D)) * (2.0 * NK / K) / np.sqrt(D) / s
    cat = np.ascontiguousarray(stack.swapaxes(1, 2)).reshape(-1, O)
    words, scales = pack_weight(cat, "e4m3")
    return {"neighbourhood_features": neighbourhood_features,
            "region_relation_weights": region_relation_weights,
            "mean_relation": mean_relation,
            "precision_relation": precision_relation,
            "W_words": words,
            "W_scales": scales}


def reference(neighbourhood_features, region_relation_weights, mean_relation, precision_relation, W_words, W_scales):
    feat = f64(neighbourhood_features)
    b, k, d = feat.shape
    diff = (f64(region_relation_weights)[..., None] - f64(mean_relation)) ** 2
    w = np.exp(-0.5 * diff / (1e-14 + f64(precision_relation) ** 2))
    w = w / np.sum(w, axis=-1, keepdims=True)
    ws = np.sum(w, axis=2)
    weighted = ws[..., None] * feat[:, :, None, :]
    a = mxq(weighted, 3, "e4m3").transpose(2, 0, 1, 3).reshape(NK, b * k, d)
    wq = unpack_weight(W_words, W_scales, "e4m3").reshape(NK, D, O)
    out = a @ wq
    return out.transpose(1, 0, 2).reshape(b, k, -1)

@@ -1,0 +1,265 @@
+from contextlib import ExitStack
+
+import concourse.mybir as mybir
+from concourse.masks import make_identity
+
+F32 = mybir.dt.float32
+BF16 = mybir.dt.bfloat16
+I32 = mybir.dt.int32
+U32 = mybir.dt.uint32
+U8 = mybir.dt.uint8
+FP8X4 = mybir.dt.float8_e4m3fn_x4
+ALU = mybir.AluOpType
+ACT = mybir.ActivationFunctionType
+AXIS = mybir.AxisListType
+
+P = 128
+ROWS = 160 * 36
+TILES = ROWS // P
+NEIGHBOURS = 36
+D = 512
+NK = 4
+O = 256
+PACK = 4
+WORDS = D // 2
+BANK = 512
+CHUNK = 5
+CHUNKS = TILES // CHUNK
+VECTOR_DRAIN_STEPS = 2
+
+FLOPS = 2 * ROWS * D * O * NK
+
+
+def tile_visualconvolution_t_e_kernel(
+    tc,
+    neighbourhood_features,
+    region_relation_weights,
+    mean_relation,
+    precision_relation,
+    W_words,
+    W_scales,
+    out,
+):
+    nc = tc.nc
+    feat_rows = neighbourhood_features.rearrange("b i d -> (b i) d").rearrange(
+        "(p t) d -> p t d", t=TILES
+    )
+    rel_rows = region_relation_weights.rearrange("b i j -> (b i) j").rearrange(
+        "(p t) j -> p t j", t=TILES
+    )
+    out_rows = out.rearrange("b i o -> (b i) o").rearrange("(p t) o -> p t o", t=TILES)
+
+    with ExitStack() as ctx:
+        ctx.enter_context(tc.manual_schedule())
+        const = ctx.enter_context(tc.tile_pool(name="const", bufs=1))
+        weights = ctx.enter_context(tc.tile_pool(name="weights", bufs=3))
+        stream = ctx.enter_context(tc.tile_pool(name="stream", bufs=3))
+        results = ctx.enter_context(tc.tile_pool(name="results", bufs=4))
+        turned_psum = ctx.enter_context(tc.psum_pool(name="turned_psum", bufs=4))
+        product_psum = ctx.enter_context(tc.psum_pool(name="product_psum", bufs=4))
+
+        mean_bf = const.tile([P, NK], BF16)
+        nc.scalar.dma_start(out=mean_bf[:], in_=mean_relation.partition_broadcast(P))
+        prec_bf = const.tile([P, NK], BF16)
+        nc.scalar.dma_start(out=prec_bf[:], in_=precision_relation.partition_broadcast(P))
+
+        rel_sb = const.tile([P, TILES, NEIGHBOURS], BF16)
+        nc.sync.dma_start(out=rel_sb[:], in_=rel_rows)
+
+        feat_sb = []
+        for c in range(CHUNKS):
+            feat_chunk = const.tile([P, CHUNK, D], BF16, name="feat%d" % c)
+            feat_sb.append(feat_chunk)
+        nc.sync.dma_start(out=feat_sb[0][:], in_=feat_rows[:, 0:CHUNK, :])
+
+        w_planes = const.tile([P, NK, O], U8, align_bytes=64)
+        nc.vector.memset(w_planes[:].rearrange("p n o -> p (n o)").bitcast(I32), 0)
+        for r in range(4):
+            nc.sync.dma_start(
+                out=w_planes[r:P:32, :, :].bitcast(I32),
+                in_=W_scales[:, r:16:4, :].rearrange("n q o -> q n o").bitcast(I32),
+            )
+        w_codes = const.tile([P, NK, O], U32, align_bytes=64)
+        nc.sync.dma_start(
+            out=w_codes[:].bitcast(I32),
+            in_=W_words.rearrange("n p o t -> p n (o t)").bitcast(I32),
+        )
+        for c in range(1, CHUNKS):
+            nc.sync.dma_start(
+                out=feat_sb[c][:], in_=feat_rows[:, c * CHUNK : (c + 1) * CHUNK, :]
+            )
+
+        ident = const.tile([P, P], F32)
+        make_identity(nc, ident[:])
+
+        zero = const.tile([P, 1], F32)
+        nc.vector.memset(zero[:], 0.0)
+        one = const.tile([P, 1], F32)
+        nc.scalar.activation(out=one[:], in_=zero[:], func=ACT.Exp)
+
+        neg_mean = const.tile([P, NK], F32)
+        nc.vector.tensor_scalar_mul(out=neg_mean[:], in0=mean_bf[:], scalar1=-1.0)
+        exp_scale = const.tile([P, NK], F32)
+        nc.vector.tensor_tensor(out=exp_scale[:], in0=prec_bf[:], in1=prec_bf[:], op=ALU.mult)
+        nc.vector.tensor_scalar(
+            out=exp_scale[:],
+            in0=exp_scale[:],
+            scalar1=1e-14,
+            scalar2=-2.0,
+            op0=ALU.add,
+            op1=ALU.mult,
+        )
+        nc.vector.reciprocal(out=exp_scale[:], in_=exp_scale[:])
+
+        gauss_of = {}
+        pairs_of = {}
+        total_of = {}
+        ws_of = {}
+
+        def squares(c, n):
+            if n == 0:
+                gauss = weights.tile([P, NK, CHUNK, NEIGHBOURS], F32)
+                gauss_of[c] = gauss
+            nc.scalar.activation(
+                out=gauss_of[c][:, n],
+                in_=rel_sb[:, c * CHUNK : (c + 1) * CHUNK, :],
+                func=ACT.Square,
+                bias=neg_mean[:, n : n + 1],
+                scale=1.0,
+            )
+
+        def exponentials(c, n):
+            nc.scalar.activation(
+                out=gauss_of[c][:, n],
+                in_=gauss_of[c][:, n],
+                func=ACT.Exp,
+                scale=exp_scale[:, n : n + 1],
+            )
+
+        def add_pairs(c):
+            g = gauss_of[c][:].rearrange("p n t j -> p n (t j)")
+            pairs = weights.tile([P, 2, CHUNK * NEIGHBOURS], F32)
+            pairs_of[c] = pairs
+            nc.vector.tensor_tensor(out=pairs[:], in0=g[:, 0:2], in1=g[:, 2:4], op=ALU.add)
+
+        def add_all(c):
+            total = weights.tile([P, CHUNK * NEIGHBOURS], F32)
+            total_of[c] = total
+            nc.vector.tensor_tensor(
+                out=total[:], in0=pairs_of[c][:, 0], in1=pairs_of[c][:, 1], op=ALU.add
+            )
+
+        def invert(c):
+            nc.vector.reciprocal(out=pairs_of[c][:, 0], in_=total_of[c][:])
+
+        def normalise(c):
+            g = gauss_of[c][:].rearrange("p n t j -> p n (t j)")
+            inverse = pairs_of[c][:, 0:1].to_broadcast([P, NK, CHUNK * NEIGHBOURS])
+            nc.vector.tensor_tensor(out=g, in0=g, in1=inverse, op=ALU.mult)
+
+        def sum_neighbours(c):
+            ws = weights.tile([P, NK, CHUNK], F32)
+            ws_of[c] = ws
+            nc.vector.tensor_reduce(
+                out=ws[:].rearrange("p n t -> p (n t)"),
+                in_=gauss_of[c][:].rearrange("p n t j -> p (n t) j"),
+                axis=AXIS.X,
+                op=ALU.add,
+            )
+
+        vector_steps = [add_pairs, add_all, invert, normalise, sum_neighbours]
+        assert len(vector_steps) == CHUNK and NK < CHUNK
+
+        scaled_of = {}
+        turned_of = {}
+        grouped_of = {}
+        codes_of = {}
+        planes_of = {}
+        product_of = {}
+
+        def scale(k):
+            c, t = divmod(k, CHUNK)
+            scaled = stream.tile([P, NK, D], BF16)
+            scaled_of[k] = scaled
+            for n in range(NK):
+                nc.vector.tensor_scalar_mul(
+                    out=scaled[:, n, :], in0=feat_sb[c][:, t, :], scalar1=ws_of[c][:, n, t : t + 1]
+                )
+
+        def turn(k):
+            words = scaled_of[k][:].bitcast(F32).rearrange("p n (q u) -> p n q u", u=2)
+            turned_of[k] = []
+            for b in range(2):
+                turned = turned_psum.tile([P, 2, 2, P], F32)
+                turned_of[k].append(turned)
+                for h in range(2):
+                    for u in range(2):
+                        nc.tensor.transpose(turned[:, h, u, :], words[:, 2 * b + h, :, u], ident[:])
+
+        def regroup(k):
+            grouped = stream.tile([P, NK * P * PACK], BF16, align_bytes=64)
+            grouped_of[k] = grouped
+            pairs_view = grouped[:].bitcast(F32).rearrange("p (n r u) -> p n r u", n=NK, u=2)
+            for b in range(2):
+                nc.scalar.copy(
+                    out=pairs_view[:, 2 * b : 2 * b + 2],
+                    in_=turned_of[k][b][:].rearrange("p h u r -> p h r u"),
+                )
+
+        def quantise(k):
+            codes = stream.tile([P, NK * P], U32, align_bytes=64)
+            planes = stream.tile([P, NK * P], U8, align_bytes=64)
+            codes_of[k] = codes
+            planes_of[k] = planes
+            nc.vector.quantize_mx(
+                out=codes[:].bitcast(FP8X4), scales=planes[:], in_=grouped_of[k][:]
+            )
+
+        def multiply(k):
+            product_of[k] = []
+            for b in range(2):
+                product = product_psum.tile([P, 2, O], F32)
+                product_of[k].append(product)
+                for h in range(2):
+                    n = 2 * b + h
+                    nc.tensor.matmul_mx(
+                        out=product[:, h, :],
+                        lhsT=codes_of[k][:, n * P : (n + 1) * P].bitcast(FP8X4),
+                        lhsT_scale=planes_of[k][:, n * P : (n + 1) * P],
+                        rhs=w_codes[:, n, :].bitcast(FP8X4),
+                        rhs_scale=w_planes[:, n, :],
+                        start=True,
+                        stop=True,
+                    )
+
+        def drain(k, vector_helps):
+            result = results.tile([P, NK * O], F32)
+            nc.scalar.copy(
+                out=result[:, 0:BANK], in_=product_of[k][0][:].rearrange("p h o -> p (h o)")
+            )
+            second = product_of[k][1][:].rearrange("p h o -> p (h o)")
+            if vector_helps:
+                nc.vector.tensor_copy(out=result[:, BANK : 2 * BANK], in_=second)
+            else:
+                nc.scalar.copy(out=result[:, BANK : 2 * BANK], in_=second)
+            nc.sync.dma_start(out=out_rows[:, k, :], in_=result[:])
+
+        for k in range(-2 * CHUNK, TILES + 3):
+            c, step = divmod(k, CHUNK)
+            gaussians_due = c + 2 < CHUNKS and step < NK
+            if gaussians_due:
+                squares(c + 2, step)
+            if 0 <= k < TILES:
+                scale(k)
+                turn(k)
+            if 0 <= k - 1 < TILES:
+                regroup(k - 1)
+            if 0 <= k - 2 < TILES:
+                quantise(k - 2)
+                multiply(k - 2)
+            if 0 <= c + 1 < CHUNKS:
+                vector_steps[step](c + 1)
+            if 0 <= k - 3 < TILES:
+                drain(k - 3, vector_helps=step < VECTOR_DRAIN_STEPS)
+            if gaussians_due:
+                exponentials(c + 2, step)

@@ -25,7 +25,8 @@ WORDS = D // 2
 BANK = 512
 CHUNK = 5
 CHUNKS = TILES // CHUNK
-VECTOR_DRAIN_STEPS = 2
+GAUSS_LEAD = 2
+VECTOR_DRAIN_STEPS = 3
 
 FLOPS = 2 * ROWS * D * O * NK
 
@@ -52,6 +53,7 @@ def tile_visualconvolution_t_e_kernel(
     with ExitStack() as ctx:
         ctx.enter_context(tc.manual_schedule())
         const = ctx.enter_context(tc.tile_pool(name="const", bufs=1))
+        gaussians = ctx.enter_context(tc.tile_pool(name="gaussians", bufs=GAUSS_LEAD + 2))
         weights = ctx.enter_context(tc.tile_pool(name="weights", bufs=3))
         stream = ctx.enter_context(tc.tile_pool(name="stream", bufs=3))
         results = ctx.enter_context(tc.tile_pool(name="results", bufs=4))
@@ -63,14 +65,20 @@ def tile_visualconvolution_t_e_kernel(
         prec_bf = const.tile([P, NK], BF16)
         nc.scalar.dma_start(out=prec_bf[:], in_=precision_relation.partition_broadcast(P))
 
-        rel_sb = const.tile([P, TILES, NEIGHBOURS], BF16)
-        nc.sync.dma_start(out=rel_sb[:], in_=rel_rows)
-
+        rel_sb = []
         feat_sb = []
         for c in range(CHUNKS):
+            rel_chunk = const.tile([P, CHUNK, NEIGHBOURS], BF16, name="rel%d" % c)
+            rel_sb.append(rel_chunk)
             feat_chunk = const.tile([P, CHUNK, D], BF16, name="feat%d" % c)
             feat_sb.append(feat_chunk)
-        nc.sync.dma_start(out=feat_sb[0][:], in_=feat_rows[:, 0:CHUNK, :])
+
+        def load_chunk(c):
+            tiles = slice(c * CHUNK, (c + 1) * CHUNK)
+            nc.sync.dma_start(out=rel_sb[c][:], in_=rel_rows[:, tiles, :])
+            nc.sync.dma_start(out=feat_sb[c][:], in_=feat_rows[:, tiles, :])
+
+        load_chunk(0)
 
         w_planes = const.tile([P, NK, O], U8, align_bytes=64)
         nc.vector.memset(w_planes[:].rearrange("p n o -> p (n o)").bitcast(I32), 0)
@@ -85,9 +93,7 @@ def tile_visualconvolution_t_e_kernel(
             in_=W_words.rearrange("n p o t -> p n (o t)").bitcast(I32),
         )
         for c in range(1, CHUNKS):
-            nc.sync.dma_start(
-                out=feat_sb[c][:], in_=feat_rows[:, c * CHUNK : (c + 1) * CHUNK, :]
-            )
+            load_chunk(c)
 
         ident = const.tile([P, P], F32)
         make_identity(nc, ident[:])
@@ -118,11 +124,11 @@ def tile_visualconvolution_t_e_kernel(
 
         def squares(c, n):
             if n == 0:
-                gauss = weights.tile([P, NK, CHUNK, NEIGHBOURS], F32)
+                gauss = gaussians.tile([P, NK, CHUNK, NEIGHBOURS], F32)
                 gauss_of[c] = gauss
             nc.scalar.activation(
                 out=gauss_of[c][:, n],
-                in_=rel_sb[:, c * CHUNK : (c + 1) * CHUNK, :],
+                in_=rel_sb[c][:],
                 func=ACT.Square,
                 bias=neg_mean[:, n : n + 1],
                 scale=1.0,
@@ -244,11 +250,11 @@ def tile_visualconvolution_t_e_kernel(
                 nc.scalar.copy(out=result[:, BANK : 2 * BANK], in_=second)
             nc.sync.dma_start(out=out_rows[:, k, :], in_=result[:])
 
-        for k in range(-2 * CHUNK, TILES + 3):
+        for k in range(-GAUSS_LEAD * CHUNK, TILES + 3):
             c, step = divmod(k, CHUNK)
-            gaussians_due = c + 2 < CHUNKS and step < NK
+            gaussians_due = c + GAUSS_LEAD < CHUNKS and step < NK
             if gaussians_due:
-                squares(c + 2, step)
+                squares(c + GAUSS_LEAD, step)
             if 0 <= k < TILES:
                 scale(k)
                 turn(k)
@@ -260,6 +266,6 @@ def tile_visualconvolution_t_e_kernel(
             if 0 <= c + 1 < CHUNKS:
                 vector_steps[step](c + 1)
             if 0 <= k - 3 < TILES:
-                drain(k - 3, vector_helps=step < VECTOR_DRAIN_STEPS)
+                drain(k - 3, vector_helps=step < VECTOR_DRAIN_STEPS or k >= TILES)
             if gaussians_due:
-                exponentials(c + 2, step)
+                exponentials(c + GAUSS_LEAD, step)

@@ -25,7 +25,6 @@ WORDS = D // 2
 BANK = 512
 CHUNK = 5
 CHUNKS = TILES // CHUNK
-GAUSS_LEAD = 2
 VECTOR_DRAIN_STEPS = 3
 
 FLOPS = 2 * ROWS * D * O * NK
@@ -53,12 +52,13 @@ def tile_visualconvolution_t_e_kernel(
     with ExitStack() as ctx:
         ctx.enter_context(tc.manual_schedule())
         const = ctx.enter_context(tc.tile_pool(name="const", bufs=1))
-        gaussians = ctx.enter_context(tc.tile_pool(name="gaussians", bufs=GAUSS_LEAD + 2))
+        gaussians = ctx.enter_context(tc.tile_pool(name="gaussians", bufs=4))
         weights = ctx.enter_context(tc.tile_pool(name="weights", bufs=3))
         stream = ctx.enter_context(tc.tile_pool(name="stream", bufs=3))
         results = ctx.enter_context(tc.tile_pool(name="results", bufs=4))
-        turned_psum = ctx.enter_context(tc.psum_pool(name="turned_psum", bufs=4))
+        turned_psum = ctx.enter_context(tc.psum_pool(name="turned_psum", bufs=3))
         product_psum = ctx.enter_context(tc.psum_pool(name="product_psum", bufs=4))
+        total_psum = ctx.enter_context(tc.psum_pool(name="total_psum", bufs=1))
 
         mean_bf = const.tile([P, NK], BF16)
         nc.scalar.dma_start(out=mean_bf[:], in_=mean_relation.partition_broadcast(P))
@@ -118,8 +118,8 @@ def tile_visualconvolution_t_e_kernel(
         nc.vector.reciprocal(out=exp_scale[:], in_=exp_scale[:])
 
         gauss_of = {}
-        pairs_of = {}
         total_of = {}
+        inverse_of = {}
         ws_of = {}
 
         def squares(c, n):
@@ -142,25 +142,26 @@ def tile_visualconvolution_t_e_kernel(
                 scale=exp_scale[:, n : n + 1],
             )
 
-        def add_pairs(c):
-            g = gauss_of[c][:].rearrange("p n t j -> p n (t j)")
-            pairs = weights.tile([P, 2, CHUNK * NEIGHBOURS], F32)
-            pairs_of[c] = pairs
-            nc.vector.tensor_tensor(out=pairs[:], in0=g[:, 0:2], in1=g[:, 2:4], op=ALU.add)
-
-        def add_all(c):
-            total = weights.tile([P, CHUNK * NEIGHBOURS], F32)
-            total_of[c] = total
-            nc.vector.tensor_tensor(
-                out=total[:], in0=pairs_of[c][:, 0], in1=pairs_of[c][:, 1], op=ALU.add
+        def add_gaussians(c, n):
+            if n == 0:
+                total = total_psum.tile([P, CHUNK * NEIGHBOURS], F32)
+                total_of[c] = total
+            nc.tensor.matmul(
+                out=total_of[c][:],
+                lhsT=ident[:],
+                rhs=gauss_of[c][:, n].rearrange("p t j -> p (t j)"),
+                start=(n == 0),
+                stop=(n == NK - 1),
             )
 
         def invert(c):
-            nc.vector.reciprocal(out=pairs_of[c][:, 0], in_=total_of[c][:])
+            inverse = weights.tile([P, 1, CHUNK * NEIGHBOURS], F32)
+            inverse_of[c] = inverse
+            nc.vector.reciprocal(out=inverse[:, 0, :], in_=total_of[c][:])
 
         def normalise(c):
             g = gauss_of[c][:].rearrange("p n t j -> p n (t j)")
-            inverse = pairs_of[c][:, 0:1].to_broadcast([P, NK, CHUNK * NEIGHBOURS])
+            inverse = inverse_of[c][:].to_broadcast([P, NK, CHUNK * NEIGHBOURS])
             nc.vector.tensor_tensor(out=g, in0=g, in1=inverse, op=ALU.mult)
 
         def sum_neighbours(c):
@@ -173,8 +174,8 @@ def tile_visualconvolution_t_e_kernel(
                 op=ALU.add,
             )
 
-        vector_steps = [add_pairs, add_all, invert, normalise, sum_neighbours]
-        assert len(vector_steps) == CHUNK and NK < CHUNK
+        vector_steps = [invert, normalise, sum_neighbours]
+        assert len(vector_steps) <= CHUNK and NK < CHUNK
 
         scaled_of = {}
         turned_of = {}
@@ -250,22 +251,23 @@ def tile_visualconvolution_t_e_kernel(
                 nc.scalar.copy(out=result[:, BANK : 2 * BANK], in_=second)
             nc.sync.dma_start(out=out_rows[:, k, :], in_=result[:])
 
-        for k in range(-GAUSS_LEAD * CHUNK, TILES + 3):
+        for k in range(-2 * CHUNK, TILES + 3):
             c, step = divmod(k, CHUNK)
-            gaussians_due = c + GAUSS_LEAD < CHUNKS and step < NK
-            if gaussians_due:
-                squares(c + GAUSS_LEAD, step)
+            if c + 2 < CHUNKS and step < NK:
+                squares(c + 2, step)
+            if 0 <= k - 1 < TILES:
+                regroup(k - 1)
+            if c + 2 < CHUNKS and step >= 1:
+                add_gaussians(c + 2, step - 1)
             if 0 <= k < TILES:
                 scale(k)
                 turn(k)
-            if 0 <= k - 1 < TILES:
-                regroup(k - 1)
             if 0 <= k - 2 < TILES:
                 quantise(k - 2)
                 multiply(k - 2)
-            if 0 <= c + 1 < CHUNKS:
+            if 0 <= c + 1 < CHUNKS and step < len(vector_steps):
                 vector_steps[step](c + 1)
             if 0 <= k - 3 < TILES:
-                drain(k - 3, vector_helps=step < VECTOR_DRAIN_STEPS or k >= TILES)
-            if gaussians_due:
-                exponentials(c + GAUSS_LEAD, step)
+                drain(k - 3, vector_helps=step >= CHUNK - VECTOR_DRAIN_STEPS or k >= TILES)
+            if c + 2 < CHUNKS and step < NK:
+                exponentials(c + 2, step)

@@ -190,18 +190,20 @@ def tile_visualconvolution_t_e_kernel(
             scaled_of[k] = scaled
             for n in range(NK):
                 nc.vector.tensor_scalar_mul(
-                    out=scaled[:, n, :], in0=feat_sb[c][:, t, :], scalar1=ws_of[c][:, n, t : t + 1]
+                    out=scaled[:, n, :].rearrange("p (u q e) -> p q u e", u=2, e=2),
+                    in0=feat_sb[c][:, t, :].rearrange("p (q u e) -> p q u e", u=2, e=2),
+                    scalar1=ws_of[c][:, n, t : t + 1],
                 )
 
         def turn(k):
-            words = scaled_of[k][:].bitcast(F32).rearrange("p n (q u) -> p n q u", u=2)
+            words = scaled_of[k][:].bitcast(F32).rearrange("p n (u q) -> p n u q", u=2)
             turned_of[k] = []
             for b in range(2):
                 turned = turned_psum.tile([P, 2, 2, P], F32)
                 turned_of[k].append(turned)
                 for h in range(2):
                     for u in range(2):
-                        nc.tensor.transpose(turned[:, h, u, :], words[:, 2 * b + h, :, u], ident[:])
+                        nc.tensor.transpose(turned[:, h, u, :], words[:, 2 * b + h, u, :], ident[:])
 
         def regroup(k):
             grouped = stream.tile([P, NK * P * PACK], BF16, align_bytes=64)

@@ -27,6 +27,8 @@ CHUNK = 5
 CHUNKS = TILES // CHUNK
 VECTOR_DRAIN_STEPS = 3
 
+WARM_UP = 13
+
 FLOPS = 2 * ROWS * D * O * NK
 
 
@@ -60,10 +62,10 @@ def tile_visualconvolution_t_e_kernel(
         product_psum = ctx.enter_context(tc.psum_pool(name="product_psum", bufs=4))
         total_psum = ctx.enter_context(tc.psum_pool(name="total_psum", bufs=1))
 
-        mean_bf = const.tile([P, NK], BF16)
-        nc.scalar.dma_start(out=mean_bf[:], in_=mean_relation.partition_broadcast(P))
         prec_bf = const.tile([P, NK], BF16)
         nc.scalar.dma_start(out=prec_bf[:], in_=precision_relation.partition_broadcast(P))
+        mean_bf = const.tile([P, NK], BF16)
+        nc.scalar.dma_start(out=mean_bf[:], in_=mean_relation.partition_broadcast(P))
 
         rel_sb = []
         feat_sb = []
@@ -98,13 +100,19 @@ def tile_visualconvolution_t_e_kernel(
         ident = const.tile([P, P], F32)
         make_identity(nc, ident[:])
 
+        warm = const.tile([P, BANK], BF16)
+        nc.vector.memset(warm[:], 0.0)
+        warm_out = product_psum.tile([P, BANK], F32, name="product")
+        for i in range(WARM_UP):
+            nc.tensor.matmul(
+                out=warm_out[:], lhsT=warm[:, 0:P], rhs=warm[:], start=True, stop=True
+            )
+
         zero = const.tile([P, 1], F32)
         nc.vector.memset(zero[:], 0.0)
         one = const.tile([P, 1], F32)
         nc.scalar.activation(out=one[:], in_=zero[:], func=ACT.Exp)
 
-        neg_mean = const.tile([P, NK], F32)
-        nc.vector.tensor_scalar_mul(out=neg_mean[:], in0=mean_bf[:], scalar1=-1.0)
         exp_scale = const.tile([P, NK], F32)
         nc.vector.tensor_tensor(out=exp_scale[:], in0=prec_bf[:], in1=prec_bf[:], op=ALU.mult)
         nc.vector.tensor_scalar(
@@ -130,8 +138,8 @@ def tile_visualconvolution_t_e_kernel(
                 out=gauss_of[c][:, n],
                 in_=rel_sb[c][:],
                 func=ACT.Square,
-                bias=neg_mean[:, n : n + 1],
-                scale=1.0,
+                bias=mean_bf[:, n : n + 1],
+                scale=-1.0,
             )
 
         def exponentials(c, n):
@@ -270,6 +278,6 @@ def tile_visualconvolution_t_e_kernel(
             if 0 <= c + 1 < CHUNKS and step < len(vector_steps):
                 vector_steps[step](c + 1)
             if 0 <= k - 3 < TILES:
-                drain(k - 3, vector_helps=step >= CHUNK - VECTOR_DRAIN_STEPS or k >= TILES)
+                drain(k - 3, vector_helps=step >= CHUNK - VECTOR_DRAIN_STEPS or c + 1 >= CHUNKS)
             if c + 2 < CHUNKS and step < NK:
                 exponentials(c + 2, step)

@@ -54,7 +54,7 @@ def tile_visualconvolution_t_e_kernel(
     with ExitStack() as ctx:
         ctx.enter_context(tc.manual_schedule())
         const = ctx.enter_context(tc.tile_pool(name="const", bufs=1))
-        gaussians = ctx.enter_context(tc.tile_pool(name="gaussians", bufs=4))
+        gaussians = ctx.enter_context(tc.tile_pool(name="gaussians", bufs=5))
         weights = ctx.enter_context(tc.tile_pool(name="weights", bufs=3))
         stream = ctx.enter_context(tc.tile_pool(name="stream", bufs=3))
         results = ctx.enter_context(tc.tile_pool(name="results", bufs=4))
@@ -75,12 +75,16 @@ def tile_visualconvolution_t_e_kernel(
             feat_chunk = const.tile([P, CHUNK, D], BF16, name="feat%d" % c)
             feat_sb.append(feat_chunk)
 
-        def load_chunk(c):
-            tiles = slice(c * CHUNK, (c + 1) * CHUNK)
-            nc.sync.dma_start(out=rel_sb[c][:], in_=rel_rows[:, tiles, :])
-            nc.sync.dma_start(out=feat_sb[c][:], in_=feat_rows[:, tiles, :])
+        def load_rel(c):
+            nc.sync.dma_start(out=rel_sb[c][:], in_=rel_rows[:, c * CHUNK : (c + 1) * CHUNK, :])
 
-        load_chunk(0)
+        def load_feat(c):
+            nc.sync.dma_start(out=feat_sb[c][:], in_=feat_rows[:, c * CHUNK : (c + 1) * CHUNK, :])
+
+        load_rel(0)
+        load_rel(1)
+        load_rel(2)
+        load_feat(0)
 
         w_planes = const.tile([P, NK, O], U8, align_bytes=64)
         nc.vector.memset(w_planes[:].rearrange("p n o -> p (n o)").bitcast(I32), 0)
@@ -95,7 +99,9 @@ def tile_visualconvolution_t_e_kernel(
             in_=W_words.rearrange("n p o t -> p n (o t)").bitcast(I32),
         )
         for c in range(1, CHUNKS):
-            load_chunk(c)
+            if c + 2 < CHUNKS:
+                load_rel(c + 2)
+            load_feat(c)
 
         ident = const.tile([P, P], F32)
         make_identity(nc, ident[:])
@@ -261,23 +267,25 @@ def tile_visualconvolution_t_e_kernel(
                 nc.scalar.copy(out=result[:, BANK : 2 * BANK], in_=second)
             nc.sync.dma_start(out=out_rows[:, k, :], in_=result[:])
 
-        for k in range(-2 * CHUNK, TILES + 3):
+        for k in range(-3 * CHUNK, TILES + 3):
             c, step = divmod(k, CHUNK)
-            if c + 2 < CHUNKS and step < NK:
-                squares(c + 2, step)
+            if c + 3 < CHUNKS and step < NK:
+                squares(c + 3, step)
             if 0 <= k - 1 < TILES:
                 regroup(k - 1)
-            if c + 2 < CHUNKS and step >= 1:
+            if 0 <= c + 2 < CHUNKS and step >= 1:
                 add_gaussians(c + 2, step - 1)
-            if 0 <= k < TILES:
-                scale(k)
-                turn(k)
             if 0 <= k - 2 < TILES:
                 quantise(k - 2)
+            if 0 <= k + 1 < TILES:
+                scale(k + 1)
+            if 0 <= k < TILES:
+                turn(k)
+            if 0 <= k - 2 < TILES:
                 multiply(k - 2)
             if 0 <= c + 1 < CHUNKS and step < len(vector_steps):
                 vector_steps[step](c + 1)
             if 0 <= k - 3 < TILES:
                 drain(k - 3, vector_helps=step >= CHUNK - VECTOR_DRAIN_STEPS or c + 1 >= CHUNKS)
-            if c + 2 < CHUNKS and step < NK:
-                exponentials(c + 2, step)
+            if c + 3 < CHUNKS and step < NK:
+                exponentials(c + 3, step)

@@ -286,6 +286,7 @@ def tile_visualconvolution_t_e_kernel(
             if 0 <= c + 1 < CHUNKS and step < len(vector_steps):
                 vector_steps[step](c + 1)
             if 0 <= k - 3 < TILES:
-                drain(k - 3, vector_helps=step >= CHUNK - VECTOR_DRAIN_STEPS or c + 1 >= CHUNKS)
+                helps = VECTOR_DRAIN_STEPS if c + 3 < CHUNKS else VECTOR_DRAIN_STEPS - 1
+                drain(k - 3, vector_helps=step >= CHUNK - helps or c + 1 >= CHUNKS)
             if c + 3 < CHUNKS and step < NK:
                 exponentials(c + 3, step)

from contextlib import ExitStack

import concourse.mybir as mybir
from concourse.masks import make_identity

F32 = mybir.dt.float32
BF16 = mybir.dt.bfloat16
I32 = mybir.dt.int32
U32 = mybir.dt.uint32
U8 = mybir.dt.uint8
FP8X4 = mybir.dt.float8_e4m3fn_x4
ALU = mybir.AluOpType
ACT = mybir.ActivationFunctionType
AXIS = mybir.AxisListType

P = 128
ROWS = 160 * 36
TILES = ROWS // P
NEIGHBOURS = 36
D = 512
NK = 4
O = 256
PACK = 4
WORDS = D // 2
BANK = 512
CHUNK = 5
CHUNKS = TILES // CHUNK
VECTOR_DRAIN_STEPS = 3

WARM_UP = 13

FLOPS = 2 * ROWS * D * O * NK


def tile_visualconvolution_t_e_kernel(
    tc,
    neighbourhood_features,
    region_relation_weights,
    mean_relation,
    precision_relation,
    W_words,
    W_scales,
    out,
):
    nc = tc.nc
    feat_rows = neighbourhood_features.rearrange("b i d -> (b i) d").rearrange(
        "(p t) d -> p t d", t=TILES
    )
    rel_rows = region_relation_weights.rearrange("b i j -> (b i) j").rearrange(
        "(p t) j -> p t j", t=TILES
    )
    out_rows = out.rearrange("b i o -> (b i) o").rearrange("(p t) o -> p t o", t=TILES)

    with ExitStack() as ctx:
        ctx.enter_context(tc.manual_schedule())
        const = ctx.enter_context(tc.tile_pool(name="const", bufs=1))
        gaussians = ctx.enter_context(tc.tile_pool(name="gaussians", bufs=5))
        weights = ctx.enter_context(tc.tile_pool(name="weights", bufs=3))
        stream = ctx.enter_context(tc.tile_pool(name="stream", bufs=3))
        results = ctx.enter_context(tc.tile_pool(name="results", bufs=4))
        turned_psum = ctx.enter_context(tc.psum_pool(name="turned_psum", bufs=3))
        product_psum = ctx.enter_context(tc.psum_pool(name="product_psum", bufs=4))
        total_psum = ctx.enter_context(tc.psum_pool(name="total_psum", bufs=1))

        prec_bf = const.tile([P, NK], BF16)
        nc.scalar.dma_start(out=prec_bf[:], in_=precision_relation.partition_broadcast(P))
        mean_bf = const.tile([P, NK], BF16)
        nc.scalar.dma_start(out=mean_bf[:], in_=mean_relation.partition_broadcast(P))

        rel_sb = []
        feat_sb = []
        for c in range(CHUNKS):
            rel_chunk = const.tile([P, CHUNK, NEIGHBOURS], BF16, name="rel%d" % c)
            rel_sb.append(rel_chunk)
            feat_chunk = const.tile([P, CHUNK, D], BF16, name="feat%d" % c)
            feat_sb.append(feat_chunk)

        def load_rel(c):
            nc.sync.dma_start(out=rel_sb[c][:], in_=rel_rows[:, c * CHUNK : (c + 1) * CHUNK, :])

        def load_feat(c):
            nc.sync.dma_start(out=feat_sb[c][:], in_=feat_rows[:, c * CHUNK : (c + 1) * CHUNK, :])

        load_rel(0)
        load_rel(1)
        load_rel(2)
        load_feat(0)

        w_planes = const.tile([P, NK, O], U8, align_bytes=64)
        nc.vector.memset(w_planes[:].rearrange("p n o -> p (n o)").bitcast(I32), 0)
        for r in range(4):
            nc.sync.dma_start(
                out=w_planes[r:P:32, :, :].bitcast(I32),
                in_=W_scales[:, r:16:4, :].rearrange("n q o -> q n o").bitcast(I32),
            )
        w_codes = const.tile([P, NK, O], U32, align_bytes=64)
        nc.sync.dma_start(
            out=w_codes[:].bitcast(I32),
            in_=W_words.rearrange("n p o t -> p n (o t)").bitcast(I32),
        )
        for c in range(1, CHUNKS):
            if c + 2 < CHUNKS:
                load_rel(c + 2)
            load_feat(c)

        ident = const.tile([P, P], F32)
        make_identity(nc, ident[:])

        warm = const.tile([P, BANK], BF16)
        nc.vector.memset(warm[:], 0.0)
        warm_out = product_psum.tile([P, BANK], F32, name="product")
        for i in range(WARM_UP):
            nc.tensor.matmul(
                out=warm_out[:], lhsT=warm[:, 0:P], rhs=warm[:], start=True, stop=True
            )

        zero = const.tile([P, 1], F32)
        nc.vector.memset(zero[:], 0.0)
        one = const.tile([P, 1], F32)
        nc.scalar.activation(out=one[:], in_=zero[:], func=ACT.Exp)

        exp_scale = const.tile([P, NK], F32)
        nc.vector.tensor_tensor(out=exp_scale[:], in0=prec_bf[:], in1=prec_bf[:], op=ALU.mult)
        nc.vector.tensor_scalar(
            out=exp_scale[:],
            in0=exp_scale[:],
            scalar1=1e-14,
            scalar2=-2.0,
            op0=ALU.add,
            op1=ALU.mult,
        )
        nc.vector.reciprocal(out=exp_scale[:], in_=exp_scale[:])

        gauss_of = {}
        total_of = {}
        inverse_of = {}
        ws_of = {}

        def squares(c, n):
            if n == 0:
                gauss = gaussians.tile([P, NK, CHUNK, NEIGHBOURS], F32)
                gauss_of[c] = gauss
            nc.scalar.activation(
                out=gauss_of[c][:, n],
                in_=rel_sb[c][:],
                func=ACT.Square,
                bias=mean_bf[:, n : n + 1],
                scale=-1.0,
            )

        def exponentials(c, n):
            nc.scalar.activation(
                out=gauss_of[c][:, n],
                in_=gauss_of[c][:, n],
                func=ACT.Exp,
                scale=exp_scale[:, n : n + 1],
            )

        def add_gaussians(c, n):
            if n == 0:
                total = total_psum.tile([P, CHUNK * NEIGHBOURS], F32)
                total_of[c] = total
            nc.tensor.matmul(
                out=total_of[c][:],
                lhsT=ident[:],
                rhs=gauss_of[c][:, n].rearrange("p t j -> p (t j)"),
                start=(n == 0),
                stop=(n == NK - 1),
            )

        def invert(c):
            inverse = weights.tile([P, 1, CHUNK * NEIGHBOURS], F32)
            inverse_of[c] = inverse
            nc.vector.reciprocal(out=inverse[:, 0, :], in_=total_of[c][:])

        def normalise(c):
            g = gauss_of[c][:].rearrange("p n t j -> p n (t j)")
            inverse = inverse_of[c][:].to_broadcast([P, NK, CHUNK * NEIGHBOURS])
            nc.vector.tensor_tensor(out=g, in0=g, in1=inverse, op=ALU.mult)

        def sum_neighbours(c):
            ws = weights.tile([P, NK, CHUNK], F32)
            ws_of[c] = ws
            nc.vector.tensor_reduce(
                out=ws[:].rearrange("p n t -> p (n t)"),
                in_=gauss_of[c][:].rearrange("p n t j -> p (n t) j"),
                axis=AXIS.X,
                op=ALU.add,
            )

        vector_steps = [invert, normalise, sum_neighbours]
        assert len(vector_steps) <= CHUNK and NK < CHUNK

        scaled_of = {}
        turned_of = {}
        grouped_of = {}
        codes_of = {}
        planes_of = {}
        product_of = {}

        def scale(k):
            c, t = divmod(k, CHUNK)
            scaled = stream.tile([P, NK, D], BF16)
            scaled_of[k] = scaled
            for n in range(NK):
                nc.vector.tensor_scalar_mul(
                    out=scaled[:, n, :].rearrange("p (u q e) -> p q u e", u=2, e=2),
                    in0=feat_sb[c][:, t, :].rearrange("p (q u e) -> p q u e", u=2, e=2),
                    scalar1=ws_of[c][:, n, t : t + 1],
                )

        def turn(k):
            words = scaled_of[k][:].bitcast(F32).rearrange("p n (u q) -> p n u q", u=2)
            turned_of[k] = []
            for b in range(2):
                turned = turned_psum.tile([P, 2, 2, P], F32)
                turned_of[k].append(turned)
                for h in range(2):
                    for u in range(2):
                        nc.tensor.transpose(turned[:, h, u, :], words[:, 2 * b + h, u, :], ident[:])

        def regroup(k):
            grouped = stream.tile([P, NK * P * PACK], BF16, align_bytes=64)
            grouped_of[k] = grouped
            pairs_view = grouped[:].bitcast(F32).rearrange("p (n r u) -> p n r u", n=NK, u=2)
            for b in range(2):
                nc.scalar.copy(
                    out=pairs_view[:, 2 * b : 2 * b + 2],
                    in_=turned_of[k][b][:].rearrange("p h u r -> p h r u"),
                )

        def quantise(k):
            codes = stream.tile([P, NK * P], U32, align_bytes=64)
            planes = stream.tile([P, NK * P], U8, align_bytes=64)
            codes_of[k] = codes
            planes_of[k] = planes
            nc.vector.quantize_mx(
                out=codes[:].bitcast(FP8X4), scales=planes[:], in_=grouped_of[k][:]
            )

        def multiply(k):
            product_of[k] = []
            for b in range(2):
                product = product_psum.tile([P, 2, O], F32)
                product_of[k].append(product)
                for h in range(2):
                    n = 2 * b + h
                    nc.tensor.matmul_mx(
                        out=product[:, h, :],
                        lhsT=codes_of[k][:, n * P : (n + 1) * P].bitcast(FP8X4),
                        lhsT_scale=planes_of[k][:, n * P : (n + 1) * P],
                        rhs=w_codes[:, n, :].bitcast(FP8X4),
                        rhs_scale=w_planes[:, n, :],
                        start=True,
                        stop=True,
                    )

        def drain(k, vector_helps):
            result = results.tile([P, NK * O], F32)
            nc.scalar.copy(
                out=result[:, 0:BANK], in_=product_of[k][0][:].rearrange("p h o -> p (h o)")
            )
            second = product_of[k][1][:].rearrange("p h o -> p (h o)")
            if vector_helps:
                nc.vector.tensor_copy(out=result[:, BANK : 2 * BANK], in_=second)
            else:
                nc.scalar.copy(out=result[:, BANK : 2 * BANK], in_=second)
            nc.sync.dma_start(out=out_rows[:, k, :], in_=result[:])

        for k in range(-3 * CHUNK, TILES + 3):
            c, step = divmod(k, CHUNK)
            if c + 3 < CHUNKS and step < NK:
                squares(c + 3, step)
            if 0 <= k - 1 < TILES:
                regroup(k - 1)
            if 0 <= c + 2 < CHUNKS and step >= 1:
                add_gaussians(c + 2, step - 1)
            if 0 <= k - 2 < TILES:
                quantise(k - 2)
            if 0 <= k + 1 < TILES:
                scale(k + 1)
            if 0 <= k < TILES:
                turn(k)
            if 0 <= k - 2 < TILES:
                multiply(k - 2)
            if 0 <= c + 1 < CHUNKS and step < len(vector_steps):
                vector_steps[step](c + 1)
            if 0 <= k - 3 < TILES:
                helps = VECTOR_DRAIN_STEPS if c + 3 < CHUNKS else VECTOR_DRAIN_STEPS - 1
                drain(k - 3, vector_helps=step >= CHUNK - helps or c + 1 >= CHUNKS)
            if c + 3 < CHUNKS and step < NK:
                exponentials(c + 3, step)
